import numpy as np
import ml_dtypes


def mxq(x, axis, fmt="e4m3"):
    dtype, down = {"e4m3": (ml_dtypes.float8_e4m3fn, 7), "e5m2": (ml_dtypes.float8_e5m2, 14)}[fmt]
    v = np.moveaxis(np.asarray(x, np.float32).astype(ml_dtypes.bfloat16).astype(np.float64), axis, -1)
    blocks = v.reshape(v.shape[:-1] + (-1, 32))
    amax = np.abs(blocks).max(-1, keepdims=True)
    byte = np.maximum(np.where(amax > 0, np.frexp(amax)[1] - 1 + 127, 0) - down, 1)
    scale = np.exp2(byte - 127.0)
    codes = (blocks / scale).astype(np.float32).astype(dtype).astype(np.float64)
    return np.moveaxis((codes * scale).reshape(v.shape), -1, axis)


WIDE = False


def mx_kscale(k):
    if not WIDE:
        return np.ones(k)
    levels = np.array([10, -10, 5, -5, 0])
    if k % 512:
        return np.exp2(np.random.permutation(np.resize(levels, k // 32))).repeat(32)
    a = np.empty((k // 512, 16))
    for p in range(k // 512):
        a[p, :8] = np.random.permutation(np.resize(levels, 8))
        for g in range(8):
            far = levels[np.abs(levels - a[p, g]) >= 10]
            a[p, g + 8] = far[np.random.randint(len(far))]
    return np.exp2(a.ravel()).repeat(32)


BF16 = ml_dtypes.bfloat16


def bf(x):
    return np.asarray(x, np.float32).astype(BF16)


def f64(x):
    return np.asarray(x).astype(np.float64)


B, C, LL, LM, LS = 256, 512, 6, 12, 6
SOFTMAX_SCALE = 10.0


def softmax(v, axis):
    e = np.exp(v - v.max(axis=axis, keepdims=True))
    return e / e.sum(axis=axis, keepdims=True)


def corr(x, w):
    return (x.transpose(2, 0, 1) @ w.transpose(2, 1, 0)).transpose(1, 2, 0)


def setup_inputs():
    s = mx_kscale(C)[None, :, None]
    return {"left": bf(np.random.standard_normal((B, C, LL)) * 0.2 / np.sqrt(C) / s),
            "right": bf(np.random.standard_normal((B, C, LL)) * 0.2 / np.sqrt(C) / s),
            "mid": bf(np.random.standard_normal((B, C, LM)) * s),
            "sc00": bf(np.random.standard_normal((B, C, LS)) * 0.1),
            "sc01": bf(np.random.standard_normal((B, C, LS)) * 0.1),
            "sc10": bf(np.random.standard_normal((B, C, LS)) * 0.1),
            "sc11": bf(np.random.standard_normal((B, C, LS)) * 0.1)}


def reference(left, right, mid, sc00, sc01, sc10, sc11):
    left, right, mid, sc00, sc10 = f64(left), f64(right), f64(mid), f64(sc00), f64(sc10)
    Bn, Cn, Lm = mid.shape
    left_cat = np.concatenate([left, right], axis=2)
    raw0 = np.concatenate([sc00, sc10], axis=2)
    raw1 = sc10
    Ls = sc10.shape[2]
    nit = min((Lm + 1) // 2, (left_cat.shape[2] + 1) // 2, Bn)
    X0 = mxq(mid[:, :, 0:2 * nit:2], 1, "e4m3")
    X1 = mxq(mid[:, :, 1:2 * nit:2], 1, "e4m3")
    W0 = mxq(left_cat[:, :, 0:2 * nit:2], 1, "e4m3")
    W1 = mxq(left_cat[:, :, 1:2 * nit:2], 1, "e4m3")
    out0 = corr(X0, W1)
    out1 = corr(X0, W0) + corr(X1, W1)
    yi = np.stack([out0, out1], axis=-1)
    yi = softmax(yi * SOFTMAX_SCALE, 1)
    yi = np.pad(yi, ((0, 0), (0, Cn - Bn), (0, 0), (0, 0)))
    outs = []
    for raw in (raw0, raw1):
        center = raw[:, :, :nit]
        y = np.concatenate([yi, center[..., None]], axis=-1)
        y = y.reshape(Bn, Cn, 3 * nit)
        pad = Ls - 3 * nit
        if pad > 0:
            y = np.pad(y, ((0, 0), (0, 0), (0, pad)))
        outs.append(y)
    return tuple(outs)

@@ -1,0 +1,258 @@
+from contextlib import ExitStack
+
+import concourse.mybir as mybir
+from concourse.masks import make_identity
+
+F32 = mybir.dt.float32
+BF16 = mybir.dt.bfloat16
+I32 = mybir.dt.int32
+U32 = mybir.dt.uint32
+U8 = mybir.dt.uint8
+FP8X4 = mybir.dt.float8_e4m3fn_x4
+ACT = mybir.ActivationFunctionType
+ALU = mybir.AluOpType
+AXIS = mybir.AxisListType
+
+P = 128
+PACK = 4
+ROWS = 256
+ROW_TILES = ROWS // P
+C = 512
+CHUNKS = 6
+SIDE_CHUNKS = 3
+SLOTS = 3
+WIDTH = CHUNKS * SLOTS
+SOFTMAX_SCALE = 10.0
+STEP = 128
+HALVES = ROWS // STEP
+RUN = 4
+
+SIDE_UNITS = CHUNKS * ROW_TILES
+UNITS = SIDE_UNITS + ROW_TILES * CHUNKS
+AHEAD = 4
+PIECE_BUFFERS = 7
+
+FLOPS = 3 * CHUNKS * 2 * ROWS * C * ROWS
+BYTES = 2 * 6 * ROWS * C * CHUNKS + 4 * 2 * ROWS * C * WIDTH
+
+
+def tile_inpainting_kernel(tc, left, right, mid, sc00, sc01, sc10, sc11, out_0, out_1):
+    nc = tc.nc
+    centres = [sc00, sc10]
+    outs = [out_0, out_1]
+
+    def by_row_tile(dram):
+        return dram.rearrange("(r p) c s -> r p (c s)", p=P)
+
+    with ExitStack() as ctx:
+        ctx.enter_context(tc.manual_schedule())
+        keep = ctx.enter_context(tc.tile_pool(name="keep", bufs=1))
+        stage = ctx.enter_context(tc.tile_pool(name="stage", bufs=4))
+        small = ctx.enter_context(tc.tile_pool(name="small", bufs=4))
+        pieces = ctx.enter_context(tc.tile_pool(name="pieces", bufs=PIECE_BUFFERS))
+        turned_pool = ctx.enter_context(tc.psum_pool(name="turned_pool", bufs=AHEAD))
+        logit_pool = ctx.enter_context(tc.psum_pool(name="logit_pool", bufs=4))
+
+        identity = keep.tile([P, P], F32, name="identity")
+        make_identity(nc, identity[:])
+        warm = keep.tile([P, 1], F32, name="warm")
+        nc.scalar.activation(out=warm[:], in_=identity[:, 0:1], func=ACT.Exp)
+
+        upper_src = [[keep.tile([P, SLOTS, ROWS * CHUNKS], BF16, name="upper_src%d%d" % (k, r)) for r in range(ROW_TILES)] for k in range(2)]
+        lower_src = [[keep.tile([P, ROWS * CHUNKS], BF16, name="lower_src%d%d" % (k, r)) for r in range(ROW_TILES)] for k in range(2)]
+        mid_sb = [keep.tile([P, C * 2 * CHUNKS], BF16, name="mid%d" % r) for r in range(ROW_TILES)]
+        w_codes = keep.tile([P, CHUNKS, 2 * ROWS], U32, name="w_codes", align_bytes=64)
+        w_scales = keep.tile([P, CHUNKS, 2 * ROWS], U8, name="w_scales", align_bytes=64)
+        x_codes = keep.tile([P, ROW_TILES, CHUNKS, 2 * P], U32, name="x_codes", align_bytes=64)
+        x_scales = keep.tile([P, ROW_TILES, CHUNKS, 2 * P], U8, name="x_scales", align_bytes=64)
+
+        for r in range(ROW_TILES):
+            for k in range(2):
+                nc.vector.memset(upper_src[k][r][:, 0 : SLOTS - 1, :].bitcast(I32), 0)
+
+        def load_upper(k, r):
+            nc.sync.dma_start(out=upper_src[k][r][:, SLOTS - 1, :], in_=by_row_tile(centres[k])[r][:, ROWS * CHUNKS :])
+
+        def load_lower(k, r):
+            nc.sync.dma_start(out=lower_src[k][r][:], in_=by_row_tile(centres[k])[r][:, : ROWS * CHUNKS])
+
+        def store(k, r, c0, filled):
+            nc.sync.dma_start(out=by_row_tile(outs[k])[r][:, c0 * WIDTH : (c0 + STEP) * WIDTH], in_=filled[:])
+
+        def upper_piece(i):
+            r, k, h = i // (2 * HALVES), i // HALVES % 2, i % HALVES
+            filled = pieces.tile([P, STEP * WIDTH], F32, name="filled")
+            nc.vector.tensor_copy(
+                out=filled[:].rearrange("p (x j) -> p x j", j=SLOTS),
+                in_=upper_src[k][r][:, :, h * STEP * CHUNKS : (h + 1) * STEP * CHUNKS].rearrange("p j x -> p x j"),
+            )
+            store(k, r, ROWS + h * STEP, filled)
+
+        side_sb = []
+        planes = []
+        turned, w_grouped, x_grouped, logits, shifts, sums = {}, {}, {}, {}, {}, {}
+
+        def turn(n):
+            if n < SIDE_UNITS:
+                t, r = divmod(n, ROW_TILES)
+                rows_sb, chunks_held, chunk = side_sb[t // SIDE_CHUNKS][r], SIDE_CHUNKS, t % SIDE_CHUNKS
+            else:
+                r, chunk = divmod(n - SIDE_UNITS, CHUNKS)
+                rows_sb, chunks_held = mid_sb[r], CHUNKS
+            words = rows_sb[:].bitcast(F32).rearrange("p (c u i) -> p u c i", u=PACK, c=P, i=chunks_held)
+            bank = turned_pool.tile([P, PACK * P], F32, name="bank")
+            for u in range(PACK):
+                nc.tensor.transpose(bank[:, u * P : (u + 1) * P], words[:, u, :, chunk], identity[:])
+            turned[n] = bank
+
+        def empty(n):
+            if n < SIDE_UNITS:
+                t, r = divmod(n, ROW_TILES)
+                if r == 0:
+                    w_grouped[t] = stage.tile([P, 2, ROWS, PACK], BF16, name="w_grouped", align_bytes=64)
+                target = w_grouped[t][:, :, r * P : (r + 1) * P, :]
+            else:
+                x_grouped[n] = stage.tile([P, 2, P, PACK], BF16, name="x_grouped", align_bytes=64)
+                target = x_grouped[n][:]
+            nc.scalar.copy(out=target, in_=turned[n][:].bitcast(BF16).rearrange("p (u b e) -> p e b u", u=PACK, b=P, e=2))
+
+        def quantise(n):
+            if n < SIDE_UNITS:
+                t, r = divmod(n, ROW_TILES)
+                if r == ROW_TILES - 1:
+                    nc.vector.quantize_mx(
+                        out=w_codes[:, t, :].bitcast(FP8X4),
+                        scales=w_scales[:, t, :],
+                        in_=w_grouped[t][:].rearrange("p e o u -> p (e o u)"),
+                    )
+            else:
+                r, t = divmod(n - SIDE_UNITS, CHUNKS)
+                nc.vector.quantize_mx(
+                    out=x_codes[:, r, t, :].bitcast(FP8X4),
+                    scales=x_scales[:, r, t, :],
+                    in_=x_grouped[n][:].rearrange("p e b u -> p (e b u)"),
+                )
+
+        even, odd = slice(0, P), slice(P, 2 * P)
+        w_even, w_odd = slice(0, ROWS), slice(ROWS, 2 * ROWS)
+
+        def product(out, r, t, x_cols, w_cols, start, stop):
+            nc.tensor.matmul_mx(
+                out=out,
+                lhsT=x_codes[:, r, t, x_cols].bitcast(FP8X4),
+                lhsT_scale=x_scales[:, r, t, x_cols],
+                rhs=w_codes[:, t, w_cols].bitcast(FP8X4),
+                rhs_scale=w_scales[:, t, w_cols],
+                start=start,
+                stop=stop,
+            )
+
+        def products(n):
+            r, t = divmod(n - SIDE_UNITS, CHUNKS)
+            a = logit_pool.tile([P, 2, ROWS], F32, name="a")
+            product(a[:, 0, :], r, t, even, w_odd, True, True)
+            product(a[:, 1, :], r, t, even, w_even, True, False)
+            product(a[:, 1, :], r, t, odd, w_odd, False, True)
+            logits[n] = a
+
+        def exponentials(n):
+            r, t = divmod(n - SIDE_UNITS, CHUNKS)
+            sums[n] = small.tile([P, 2], F32, name="total")
+            for j in range(2):
+                nc.scalar.activation(
+                    out=planes[r][:, SLOTS * t + j, :],
+                    in_=logits[n][:, j, :],
+                    func=ACT.Exp,
+                    bias=shifts[n][:, j : j + 1],
+                    scale=SOFTMAX_SCALE,
+                    accum_out=sums[n][:, j : j + 1],
+                )
+
+        def maxima_and_gains(n_max, n_gain):
+            if SIDE_UNITS <= n_max < UNITS:
+                top = small.tile([P, 2], F32, name="top")
+                nc.vector.tensor_reduce(out=top[:], in_=logits[n_max][:], axis=AXIS.X, op=ALU.max)
+            if SIDE_UNITS <= n_gain < UNITS:
+                gain = small.tile([P, 2], F32, name="gain")
+                nc.vector.reciprocal(out=gain[:], in_=sums[n_gain][:])
+            if SIDE_UNITS <= n_max < UNITS:
+                shifts[n_max] = small.tile([P, 2], F32, name="shift")
+                nc.vector.tensor_scalar(out=shifts[n_max][:], in0=top[:], scalar1=-SOFTMAX_SCALE, scalar2=None, op0=ALU.mult)
+            if SIDE_UNITS <= n_gain < UNITS:
+                r, t = divmod(n_gain - SIDE_UNITS, CHUNKS)
+                for j in range(2):
+                    nc.vector.tensor_scalar(
+                        out=planes[r][:, SLOTS * t + j, :],
+                        in0=planes[r][:, SLOTS * t + j, :],
+                        scalar1=gain[:, j : j + 1],
+                        scalar2=None,
+                        op0=ALU.mult,
+                    )
+
+        def cast_centres(copy, r, k, h):
+            o0 = h * STEP
+            copy(
+                out=planes[r][:].rearrange("p (t j) o -> p t j o", j=SLOTS)[:, :, SLOTS - 1, o0 : o0 + STEP],
+                in_=lower_src[k][r][:, o0 * CHUNKS : (o0 + STEP) * CHUNKS].rearrange("p (o t) -> p t o", t=CHUNKS),
+            )
+
+        def lower_piece(r, k, h):
+            o0 = h * STEP
+            filled = pieces.tile([P, STEP * WIDTH], F32, name="filled")
+            nc.vector.tensor_copy(
+                out=filled[:].rearrange("p (g i s) -> p g s i", i=RUN, s=WIDTH),
+                in_=planes[r][:, :, o0 : o0 + STEP].rearrange("p s (g i) -> p g s i", i=RUN),
+            )
+            store(k, r, o0, filled)
+
+        def step(n):
+            if n < UNITS:
+                empty(n)
+            if 0 <= n - 1 < UNITS:
+                quantise(n - 1)
+                if n - 1 >= SIDE_UNITS:
+                    products(n - 1)
+            if n + AHEAD < UNITS:
+                turn(n + AHEAD)
+            maxima_and_gains(n - 2, n - 4)
+            if SIDE_UNITS <= n - 3 < UNITS:
+                exponentials(n - 3)
+            if n < SIDE_UNITS and n % ROW_TILES == 1:
+                upper_piece(2 + n // ROW_TILES)
+            if SIDE_UNITS <= n < SIDE_UNITS + ROW_TILES * HALVES:
+                cast_centres(nc.vector.tensor_copy, (n - SIDE_UNITS) // HALVES, 0, (n - SIDE_UNITS) % HALVES)
+            for r in range(ROW_TILES):
+                i = n - (SIDE_UNITS + CHUNKS * (r + 1) + 3)
+                if 1 <= i < 1 + HALVES:
+                    cast_centres(nc.scalar.copy, r, 1, i - 1)
+                if 0 <= i < 2 * HALVES:
+                    lower_piece(r, i // HALVES, i % HALVES)
+
+        with tc.tile_pool(name="sides", bufs=1) as sides:
+            for h in range(2):
+                side_sb.append([sides.tile([P, C * 2 * SIDE_CHUNKS], BF16, name="side%d%d" % (h, r)) for r in range(ROW_TILES)])
+            load_upper(0, 0)
+            for r in range(ROW_TILES):
+                nc.sync.dma_start(out=side_sb[0][r][:], in_=by_row_tile(left)[r])
+            load_upper(1, 0)
+            for r in range(ROW_TILES):
+                nc.sync.dma_start(out=side_sb[1][r][:], in_=by_row_tile(right)[r])
+            load_upper(0, 1)
+            load_upper(1, 1)
+            nc.sync.dma_start(out=mid_sb[0][:], in_=by_row_tile(mid)[0])
+            load_lower(0, 0)
+            upper_piece(0)
+            upper_piece(1)
+            load_lower(0, 1)
+            nc.sync.dma_start(out=mid_sb[1][:], in_=by_row_tile(mid)[1])
+            load_lower(1, 0)
+            load_lower(1, 1)
+            for n in range(AHEAD):
+                turn(n)
+            for n in range(SIDE_UNITS - AHEAD):
+                step(n)
+        planes_pool = ctx.enter_context(tc.tile_pool(name="planes_pool", bufs=1))
+        for r in range(ROW_TILES):
+            planes.append(planes_pool.tile([P, WIDTH, ROWS], F32, name="planes%d" % r))
+        for n in range(SIDE_UNITS - AHEAD, UNITS + 3 + 2 * HALVES):
+            step(n)

@@ -26,6 +26,7 @@ SOFTMAX_SCALE = 10.0
 STEP = 128
 HALVES = ROWS // STEP
 RUN = 4
+PAIR = 2
 
 SIDE_UNITS = CHUNKS * ROW_TILES
 UNITS = SIDE_UNITS + ROW_TILES * CHUNKS
@@ -55,6 +56,11 @@ def tile_inpainting_kernel(tc, left, right, mid, sc00, sc01, sc10, sc11, out_0, 
 
         identity = keep.tile([P, P], F32, name="identity")
         make_identity(nc, identity[:])
+        reorder = keep.tile([P, P], F32, name="reorder")
+        nc.vector.tensor_copy(
+            out=reorder[:].rearrange("p (g e i) -> p g e i", e=PAIR, i=RUN),
+            in_=identity[:].rearrange("p (g i e) -> p g e i", e=PAIR, i=RUN),
+        )
         warm = keep.tile([P, 1], F32, name="warm")
         nc.scalar.activation(out=warm[:], in_=identity[:, 0:1], func=ACT.Exp)
 
@@ -95,14 +101,14 @@ def tile_inpainting_kernel(tc, left, right, mid, sc00, sc01, sc10, sc11, out_0, 
         def turn(n):
             if n < SIDE_UNITS:
                 t, r = divmod(n, ROW_TILES)
-                rows_sb, chunks_held, chunk = side_sb[t // SIDE_CHUNKS][r], SIDE_CHUNKS, t % SIDE_CHUNKS
+                rows_sb, chunks_held, chunk, order = side_sb[t // SIDE_CHUNKS][r], SIDE_CHUNKS, t % SIDE_CHUNKS, reorder
             else:
                 r, chunk = divmod(n - SIDE_UNITS, CHUNKS)
-                rows_sb, chunks_held = mid_sb[r], CHUNKS
+                rows_sb, chunks_held, order = mid_sb[r], CHUNKS, identity
             words = rows_sb[:].bitcast(F32).rearrange("p (c u i) -> p u c i", u=PACK, c=P, i=chunks_held)
             bank = turned_pool.tile([P, PACK * P], F32, name="bank")
             for u in range(PACK):
-                nc.tensor.transpose(bank[:, u * P : (u + 1) * P], words[:, u, :, chunk], identity[:])
+                nc.tensor.transpose(bank[:, u * P : (u + 1) * P], words[:, u, :, chunk], order[:])
             turned[n] = bank
 
         def empty(n):
@@ -192,16 +198,20 @@ def tile_inpainting_kernel(tc, left, right, mid, sc00, sc01, sc10, sc11, out_0, 
         def cast_centres(copy, r, k, h):
             o0 = h * STEP
             copy(
-                out=planes[r][:].rearrange("p (t j) o -> p t j o", j=SLOTS)[:, :, SLOTS - 1, o0 : o0 + STEP],
-                in_=lower_src[k][r][:, o0 * CHUNKS : (o0 + STEP) * CHUNKS].rearrange("p (o t) -> p t o", t=CHUNKS),
+                out=planes[r][:].rearrange("p (t j) o -> p t j o", j=SLOTS)[:, :, SLOTS - 1, o0 : o0 + STEP].rearrange(
+                    "p t (g e i) -> p t g e i", e=PAIR, i=RUN
+                ),
+                in_=lower_src[k][r][:, o0 * CHUNKS : (o0 + STEP) * CHUNKS].rearrange(
+                    "p (g i e t) -> p t g e i", i=RUN, e=PAIR, t=CHUNKS
+                ),
             )
 
         def lower_piece(r, k, h):
             o0 = h * STEP
             filled = pieces.tile([P, STEP * WIDTH], F32, name="filled")
             nc.vector.tensor_copy(
-                out=filled[:].rearrange("p (g i s) -> p g s i", i=RUN, s=WIDTH),
-                in_=planes[r][:, :, o0 : o0 + STEP].rearrange("p s (g i) -> p g s i", i=RUN),
+                out=filled[:].rearrange("p (g i e s) -> p g e s i", i=RUN, e=PAIR, s=WIDTH),
+                in_=planes[r][:, :, o0 : o0 + STEP].rearrange("p s (g e i) -> p g e s i", e=PAIR, i=RUN),
             )
             store(k, r, o0, filled)
 

@@ -31,7 +31,9 @@ PAIR = 2
 SIDE_UNITS = CHUNKS * ROW_TILES
 UNITS = SIDE_UNITS + ROW_TILES * CHUNKS
 AHEAD = 4
-PIECE_BUFFERS = 7
+PIECE_BUFFERS = 8
+UPPER_STEPS = (2, 3, 7, 8, 9, 13)
+CENTRE_STEPS = (15, 24)
 
 FLOPS = 3 * CHUNKS * 2 * ROWS * C * ROWS
 BYTES = 2 * 6 * ROWS * C * CHUNKS + 4 * 2 * ROWS * C * WIDTH
@@ -85,10 +87,10 @@ def tile_inpainting_kernel(tc, left, right, mid, sc00, sc01, sc10, sc11, out_0, 
         def store(k, r, c0, filled):
             nc.sync.dma_start(out=by_row_tile(outs[k])[r][:, c0 * WIDTH : (c0 + STEP) * WIDTH], in_=filled[:])
 
-        def upper_piece(i):
+        def upper_piece(copy, i):
             r, k, h = i // (2 * HALVES), i // HALVES % 2, i % HALVES
             filled = pieces.tile([P, STEP * WIDTH], F32, name="filled")
-            nc.vector.tensor_copy(
+            copy(
                 out=filled[:].rearrange("p (x j) -> p x j", j=SLOTS),
                 in_=upper_src[k][r][:, :, h * STEP * CHUNKS : (h + 1) * STEP * CHUNKS].rearrange("p j x -> p x j"),
             )
@@ -96,11 +98,16 @@ def tile_inpainting_kernel(tc, left, right, mid, sc00, sc01, sc10, sc11, out_0, 
 
         side_sb = []
         planes = []
-        turned, w_grouped, x_grouped, logits, shifts, sums = {}, {}, {}, {}, {}, {}
+        turned, w_grouped, x_grouped, logits, tops, shifts, sums, gains = {}, {}, {}, {}, {}, {}, {}, {}
+
+        def side_unit(n):
+            half, i = divmod(n, SIDE_CHUNKS * ROW_TILES)
+            r, chunk = divmod(i, SIDE_CHUNKS)
+            return half * SIDE_CHUNKS + chunk, r
 
         def turn(n):
             if n < SIDE_UNITS:
-                t, r = divmod(n, ROW_TILES)
+                t, r = side_unit(n)
                 rows_sb, chunks_held, chunk, order = side_sb[t // SIDE_CHUNKS][r], SIDE_CHUNKS, t % SIDE_CHUNKS, reorder
             else:
                 r, chunk = divmod(n - SIDE_UNITS, CHUNKS)
@@ -112,19 +119,20 @@ def tile_inpainting_kernel(tc, left, right, mid, sc00, sc01, sc10, sc11, out_0, 
             turned[n] = bank
 
         def empty(n):
+            copy = nc.vector.tensor_copy if n == 1 else nc.scalar.copy
             if n < SIDE_UNITS:
-                t, r = divmod(n, ROW_TILES)
+                t, r = side_unit(n)
                 if r == 0:
                     w_grouped[t] = stage.tile([P, 2, ROWS, PACK], BF16, name="w_grouped", align_bytes=64)
                 target = w_grouped[t][:, :, r * P : (r + 1) * P, :]
             else:
                 x_grouped[n] = stage.tile([P, 2, P, PACK], BF16, name="x_grouped", align_bytes=64)
                 target = x_grouped[n][:]
-            nc.scalar.copy(out=target, in_=turned[n][:].bitcast(BF16).rearrange("p (u b e) -> p e b u", u=PACK, b=P, e=2))
+            copy(out=target, in_=turned[n][:].bitcast(BF16).rearrange("p (u b e) -> p e b u", u=PACK, b=P, e=2))
 
         def quantise(n):
             if n < SIDE_UNITS:
-                t, r = divmod(n, ROW_TILES)
+                t, r = side_unit(n)
                 if r == ROW_TILES - 1:
                     nc.vector.quantize_mx(
                         out=w_codes[:, t, :].bitcast(FP8X4),
@@ -174,26 +182,28 @@ def tile_inpainting_kernel(tc, left, right, mid, sc00, sc01, sc10, sc11, out_0, 
                     accum_out=sums[n][:, j : j + 1],
                 )
 
-        def maxima_and_gains(n_max, n_gain):
-            if SIDE_UNITS <= n_max < UNITS:
-                top = small.tile([P, 2], F32, name="top")
-                nc.vector.tensor_reduce(out=top[:], in_=logits[n_max][:], axis=AXIS.X, op=ALU.max)
-            if SIDE_UNITS <= n_gain < UNITS:
-                gain = small.tile([P, 2], F32, name="gain")
-                nc.vector.reciprocal(out=gain[:], in_=sums[n_gain][:])
-            if SIDE_UNITS <= n_max < UNITS:
-                shifts[n_max] = small.tile([P, 2], F32, name="shift")
-                nc.vector.tensor_scalar(out=shifts[n_max][:], in0=top[:], scalar1=-SOFTMAX_SCALE, scalar2=None, op0=ALU.mult)
-            if SIDE_UNITS <= n_gain < UNITS:
-                r, t = divmod(n_gain - SIDE_UNITS, CHUNKS)
-                for j in range(2):
-                    nc.vector.tensor_scalar(
-                        out=planes[r][:, SLOTS * t + j, :],
-                        in0=planes[r][:, SLOTS * t + j, :],
-                        scalar1=gain[:, j : j + 1],
-                        scalar2=None,
-                        op0=ALU.mult,
-                    )
+        def maxima(n):
+            tops[n] = small.tile([P, 2], F32, name="top")
+            nc.vector.tensor_reduce(out=tops[n][:], in_=logits[n][:], axis=AXIS.X, op=ALU.max)
+
+        def shift(n):
+            shifts[n] = small.tile([P, 2], F32, name="shift")
+            nc.vector.tensor_scalar(out=shifts[n][:], in0=tops[n][:], scalar1=-SOFTMAX_SCALE, scalar2=None, op0=ALU.mult)
+
+        def gain(n):
+            gains[n] = small.tile([P, 2], F32, name="gain")
+            nc.vector.reciprocal(out=gains[n][:], in_=sums[n][:])
+
+        def divide(n):
+            r, t = divmod(n - SIDE_UNITS, CHUNKS)
+            for j in range(2):
+                nc.vector.tensor_scalar(
+                    out=planes[r][:, SLOTS * t + j, :],
+                    in0=planes[r][:, SLOTS * t + j, :],
+                    scalar1=gains[n][:, j : j + 1],
+                    scalar2=None,
+                    op0=ALU.mult,
+                )
 
         def cast_centres(copy, r, k, h):
             o0 = h * STEP
@@ -206,10 +216,10 @@ def tile_inpainting_kernel(tc, left, right, mid, sc00, sc01, sc10, sc11, out_0, 
                 ),
             )
 
-        def lower_piece(r, k, h):
+        def lower_piece(copy, r, k, h):
             o0 = h * STEP
             filled = pieces.tile([P, STEP * WIDTH], F32, name="filled")
-            nc.vector.tensor_copy(
+            copy(
                 out=filled[:].rearrange("p (g i e s) -> p g e s i", i=RUN, e=PAIR, s=WIDTH),
                 in_=planes[r][:, :, o0 : o0 + STEP].rearrange("p s (g e i) -> p g e s i", e=PAIR, i=RUN),
             )
@@ -224,19 +234,32 @@ def tile_inpainting_kernel(tc, left, right, mid, sc00, sc01, sc10, sc11, out_0, 
                     products(n - 1)
             if n + AHEAD < UNITS:
                 turn(n + AHEAD)
-            maxima_and_gains(n - 2, n - 4)
+            if SIDE_UNITS <= n - 4 < UNITS:
+                gain(n - 4)
+            if SIDE_UNITS <= n - 2 < UNITS:
+                maxima(n - 2)
+            if SIDE_UNITS <= n - 4 < UNITS:
+                divide(n - 4)
+            if SIDE_UNITS <= n - 2 < UNITS:
+                shift(n - 2)
             if SIDE_UNITS <= n - 3 < UNITS:
                 exponentials(n - 3)
-            if n < SIDE_UNITS and n % ROW_TILES == 1:
-                upper_piece(2 + n // ROW_TILES)
-            if SIDE_UNITS <= n < SIDE_UNITS + ROW_TILES * HALVES:
-                cast_centres(nc.vector.tensor_copy, (n - SIDE_UNITS) // HALVES, 0, (n - SIDE_UNITS) % HALVES)
+            if n in UPPER_STEPS:
+                upper_piece(nc.vector.tensor_copy, 2 + UPPER_STEPS.index(n))
             for r in range(ROW_TILES):
-                i = n - (SIDE_UNITS + CHUNKS * (r + 1) + 3)
-                if 1 <= i < 1 + HALVES:
-                    cast_centres(nc.scalar.copy, r, 1, i - 1)
-                if 0 <= i < 2 * HALVES:
-                    lower_piece(r, i // HALVES, i % HALVES)
+                if 0 <= n - CENTRE_STEPS[r] < HALVES:
+                    cast_centres(nc.vector.tensor_copy, r, 0, n - CENTRE_STEPS[r])
+            i = n - (SIDE_UNITS + CHUNKS + 3)
+            if 1 <= i < 1 + HALVES:
+                cast_centres(nc.scalar.copy, 0, 1, i - 1)
+            if 0 <= i < 2 * HALVES:
+                lower_piece(nc.scalar.copy if i == 2 * HALVES - 1 else nc.vector.tensor_copy, 0, i // HALVES, i % HALVES)
+            if n == UNITS + 3:
+                lower_piece(nc.vector.tensor_copy, 1, 0, 0)
+                lower_piece(nc.scalar.copy, 1, 0, 1)
+                for h in range(HALVES):
+                    cast_centres(nc.vector.tensor_copy, 1, 1, h)
+                    lower_piece(nc.vector.tensor_copy, 1, 1, h)
 
         with tc.tile_pool(name="sides", bufs=1) as sides:
             for h in range(2):
@@ -251,10 +274,10 @@ def tile_inpainting_kernel(tc, left, right, mid, sc00, sc01, sc10, sc11, out_0, 
             load_upper(1, 1)
             nc.sync.dma_start(out=mid_sb[0][:], in_=by_row_tile(mid)[0])
             load_lower(0, 0)
-            upper_piece(0)
-            upper_piece(1)
             load_lower(0, 1)
             nc.sync.dma_start(out=mid_sb[1][:], in_=by_row_tile(mid)[1])
+            upper_piece(nc.vector.tensor_copy, 0)
+            upper_piece(nc.scalar.copy, 1)
             load_lower(1, 0)
             load_lower(1, 1)
             for n in range(AHEAD):
@@ -264,5 +287,5 @@ def tile_inpainting_kernel(tc, left, right, mid, sc00, sc01, sc10, sc11, out_0, 
         planes_pool = ctx.enter_context(tc.tile_pool(name="planes_pool", bufs=1))
         for r in range(ROW_TILES):
             planes.append(planes_pool.tile([P, WIDTH, ROWS], F32, name="planes%d" % r))
-        for n in range(SIDE_UNITS - AHEAD, UNITS + 3 + 2 * HALVES):
+        for n in range(SIDE_UNITS - AHEAD, UNITS + 4):
             step(n)

@@ -32,6 +32,7 @@ SIDE_UNITS = CHUNKS * ROW_TILES
 UNITS = SIDE_UNITS + ROW_TILES * CHUNKS
 AHEAD = 4
 PIECE_BUFFERS = 8
+DMA_ALIGN = 256
 UPPER_STEPS = (2, 3, 7, 8, 9, 13)
 CENTRE_STEPS = (15, 24)
 
@@ -66,9 +67,9 @@ def tile_inpainting_kernel(tc, left, right, mid, sc00, sc01, sc10, sc11, out_0, 
         warm = keep.tile([P, 1], F32, name="warm")
         nc.scalar.activation(out=warm[:], in_=identity[:, 0:1], func=ACT.Exp)
 
-        upper_src = [[keep.tile([P, SLOTS, ROWS * CHUNKS], BF16, name="upper_src%d%d" % (k, r)) for r in range(ROW_TILES)] for k in range(2)]
-        lower_src = [[keep.tile([P, ROWS * CHUNKS], BF16, name="lower_src%d%d" % (k, r)) for r in range(ROW_TILES)] for k in range(2)]
-        mid_sb = [keep.tile([P, C * 2 * CHUNKS], BF16, name="mid%d" % r) for r in range(ROW_TILES)]
+        upper_src = [[keep.tile([P, SLOTS, ROWS * CHUNKS], BF16, name="upper_src%d%d" % (k, r), align_bytes=DMA_ALIGN) for r in range(ROW_TILES)] for k in range(2)]
+        lower_src = [[keep.tile([P, ROWS * CHUNKS], BF16, name="lower_src%d%d" % (k, r), align_bytes=DMA_ALIGN) for r in range(ROW_TILES)] for k in range(2)]
+        mid_sb = [keep.tile([P, C * 2 * CHUNKS], BF16, name="mid%d" % r, align_bytes=DMA_ALIGN) for r in range(ROW_TILES)]
         w_codes = keep.tile([P, CHUNKS, 2 * ROWS], U32, name="w_codes", align_bytes=64)
         w_scales = keep.tile([P, CHUNKS, 2 * ROWS], U8, name="w_scales", align_bytes=64)
         x_codes = keep.tile([P, ROW_TILES, CHUNKS, 2 * P], U32, name="x_codes", align_bytes=64)
@@ -89,7 +90,7 @@ def tile_inpainting_kernel(tc, left, right, mid, sc00, sc01, sc10, sc11, out_0, 
 
         def upper_piece(copy, i):
             r, k, h = i // (2 * HALVES), i // HALVES % 2, i % HALVES
-            filled = pieces.tile([P, STEP * WIDTH], F32, name="filled")
+            filled = pieces.tile([P, STEP * WIDTH], F32, name="filled", align_bytes=DMA_ALIGN)
             copy(
                 out=filled[:].rearrange("p (x j) -> p x j", j=SLOTS),
                 in_=upper_src[k][r][:, :, h * STEP * CHUNKS : (h + 1) * STEP * CHUNKS].rearrange("p j x -> p x j"),
@@ -218,7 +219,7 @@ def tile_inpainting_kernel(tc, left, right, mid, sc00, sc01, sc10, sc11, out_0, 
 
         def lower_piece(copy, r, k, h):
             o0 = h * STEP
-            filled = pieces.tile([P, STEP * WIDTH], F32, name="filled")
+            filled = pieces.tile([P, STEP * WIDTH], F32, name="filled", align_bytes=DMA_ALIGN)
             copy(
                 out=filled[:].rearrange("p (g i e s) -> p g e s i", i=RUN, e=PAIR, s=WIDTH),
                 in_=planes[r][:, :, o0 : o0 + STEP].rearrange("p s (g e i) -> p g e s i", e=PAIR, i=RUN),
@@ -263,7 +264,7 @@ def tile_inpainting_kernel(tc, left, right, mid, sc00, sc01, sc10, sc11, out_0, 
 
         with tc.tile_pool(name="sides", bufs=1) as sides:
             for h in range(2):
-                side_sb.append([sides.tile([P, C * 2 * SIDE_CHUNKS], BF16, name="side%d%d" % (h, r)) for r in range(ROW_TILES)])
+                side_sb.append([sides.tile([P, C * 2 * SIDE_CHUNKS], BF16, name="side%d%d" % (h, r), align_bytes=DMA_ALIGN) for r in range(ROW_TILES)])
             load_upper(0, 0)
             for r in range(ROW_TILES):
                 nc.sync.dma_start(out=side_sb[0][r][:], in_=by_row_tile(left)[r])

@@ -32,7 +32,7 @@ SIDE_UNITS = CHUNKS * ROW_TILES
 UNITS = SIDE_UNITS + ROW_TILES * CHUNKS
 AHEAD = 4
 PIECE_BUFFERS = 8
-DMA_ALIGN = 256
+DMA_ALIGN = 512
 UPPER_STEPS = (2, 3, 7, 8, 9, 13)
 CENTRE_STEPS = (15, 24)
 
@@ -127,7 +127,7 @@ def tile_inpainting_kernel(tc, left, right, mid, sc00, sc01, sc10, sc11, out_0, 
                     w_grouped[t] = stage.tile([P, 2, ROWS, PACK], BF16, name="w_grouped", align_bytes=64)
                 target = w_grouped[t][:, :, r * P : (r + 1) * P, :]
             else:
-                x_grouped[n] = stage.tile([P, 2, P, PACK], BF16, name="x_grouped", align_bytes=64)
+                x_grouped[n] = stage.tile([P, 2, P, PACK], BF16, name="x_grouped", align_bytes=64, bufs=3)
                 target = x_grouped[n][:]
             copy(out=target, in_=turned[n][:].bitcast(BF16).rearrange("p (u b e) -> p e b u", u=PACK, b=P, e=2))
 

from contextlib import ExitStack

import concourse.mybir as mybir
from concourse.masks import make_identity

F32 = mybir.dt.float32
BF16 = mybir.dt.bfloat16
I32 = mybir.dt.int32
U32 = mybir.dt.uint32
U8 = mybir.dt.uint8
FP8X4 = mybir.dt.float8_e4m3fn_x4
ACT = mybir.ActivationFunctionType
ALU = mybir.AluOpType
AXIS = mybir.AxisListType

P = 128
PACK = 4
ROWS = 256
ROW_TILES = ROWS // P
C = 512
CHUNKS = 6
SIDE_CHUNKS = 3
SLOTS = 3
WIDTH = CHUNKS * SLOTS
SOFTMAX_SCALE = 10.0
STEP = 128
HALVES = ROWS // STEP
RUN = 4
PAIR = 2

SIDE_UNITS = CHUNKS * ROW_TILES
UNITS = SIDE_UNITS + ROW_TILES * CHUNKS
AHEAD = 4
PIECE_BUFFERS = 8
DMA_ALIGN = 512
UPPER_STEPS = (2, 3, 7, 8, 9, 13)
CENTRE_STEPS = (15, 24)

FLOPS = 3 * CHUNKS * 2 * ROWS * C * ROWS
BYTES = 2 * 6 * ROWS * C * CHUNKS + 4 * 2 * ROWS * C * WIDTH


def tile_inpainting_kernel(tc, left, right, mid, sc00, sc01, sc10, sc11, out_0, out_1):
    nc = tc.nc
    centres = [sc00, sc10]
    outs = [out_0, out_1]

    def by_row_tile(dram):
        return dram.rearrange("(r p) c s -> r p (c s)", p=P)

    with ExitStack() as ctx:
        ctx.enter_context(tc.manual_schedule())
        keep = ctx.enter_context(tc.tile_pool(name="keep", bufs=1))
        stage = ctx.enter_context(tc.tile_pool(name="stage", bufs=4))
        small = ctx.enter_context(tc.tile_pool(name="small", bufs=4))
        pieces = ctx.enter_context(tc.tile_pool(name="pieces", bufs=PIECE_BUFFERS))
        turned_pool = ctx.enter_context(tc.psum_pool(name="turned_pool", bufs=AHEAD))
        logit_pool = ctx.enter_context(tc.psum_pool(name="logit_pool", bufs=4))

        identity = keep.tile([P, P], F32, name="identity")
        make_identity(nc, identity[:])
        reorder = keep.tile([P, P], F32, name="reorder")
        nc.vector.tensor_copy(
            out=reorder[:].rearrange("p (g e i) -> p g e i", e=PAIR, i=RUN),
            in_=identity[:].rearrange("p (g i e) -> p g e i", e=PAIR, i=RUN),
        )
        warm = keep.tile([P, 1], F32, name="warm")
        nc.scalar.activation(out=warm[:], in_=identity[:, 0:1], func=ACT.Exp)

        upper_src = [[keep.tile([P, SLOTS, ROWS * CHUNKS], BF16, name="upper_src%d%d" % (k, r), align_bytes=DMA_ALIGN) for r in range(ROW_TILES)] for k in range(2)]
        lower_src = [[keep.tile([P, ROWS * CHUNKS], BF16, name="lower_src%d%d" % (k, r), align_bytes=DMA_ALIGN) for r in range(ROW_TILES)] for k in range(2)]
        mid_sb = [keep.tile([P, C * 2 * CHUNKS], BF16, name="mid%d" % r, align_bytes=DMA_ALIGN) for r in range(ROW_TILES)]
        w_codes = keep.tile([P, CHUNKS, 2 * ROWS], U32, name="w_codes", align_bytes=64)
        w_scales = keep.tile([P, CHUNKS, 2 * ROWS], U8, name="w_scales", align_bytes=64)
        x_codes = keep.tile([P, ROW_TILES, CHUNKS, 2 * P], U32, name="x_codes", align_bytes=64)
        x_scales = keep.tile([P, ROW_TILES, CHUNKS, 2 * P], U8, name="x_scales", align_bytes=64)

        for r in range(ROW_TILES):
            for k in range(2):
                nc.vector.memset(upper_src[k][r][:, 0 : SLOTS - 1, :].bitcast(I32), 0)

        def load_upper(k, r):
            nc.sync.dma_start(out=upper_src[k][r][:, SLOTS - 1, :], in_=by_row_tile(centres[k])[r][:, ROWS * CHUNKS :])

        def load_lower(k, r):
            nc.sync.dma_start(out=lower_src[k][r][:], in_=by_row_tile(centres[k])[r][:, : ROWS * CHUNKS])

        def store(k, r, c0, filled):
            nc.sync.dma_start(out=by_row_tile(outs[k])[r][:, c0 * WIDTH : (c0 + STEP) * WIDTH], in_=filled[:])

        def upper_piece(copy, i):
            r, k, h = i // (2 * HALVES), i // HALVES % 2, i % HALVES
            filled = pieces.tile([P, STEP * WIDTH], F32, name="filled", align_bytes=DMA_ALIGN)
            copy(
                out=filled[:].rearrange("p (x j) -> p x j", j=SLOTS),
                in_=upper_src[k][r][:, :, h * STEP * CHUNKS : (h + 1) * STEP * CHUNKS].rearrange("p j x -> p x j"),
            )
            store(k, r, ROWS + h * STEP, filled)

        side_sb = []
        planes = []
        turned, w_grouped, x_grouped, logits, tops, shifts, sums, gains = {}, {}, {}, {}, {}, {}, {}, {}

        def side_unit(n):
            half, i = divmod(n, SIDE_CHUNKS * ROW_TILES)
            r, chunk = divmod(i, SIDE_CHUNKS)
            return half * SIDE_CHUNKS + chunk, r

        def turn(n):
            if n < SIDE_UNITS:
                t, r = side_unit(n)
                rows_sb, chunks_held, chunk, order = side_sb[t // SIDE_CHUNKS][r], SIDE_CHUNKS, t % SIDE_CHUNKS, reorder
            else:
                r, chunk = divmod(n - SIDE_UNITS, CHUNKS)
                rows_sb, chunks_held, order = mid_sb[r], CHUNKS, identity
            words = rows_sb[:].bitcast(F32).rearrange("p (c u i) -> p u c i", u=PACK, c=P, i=chunks_held)
            bank = turned_pool.tile([P, PACK * P], F32, name="bank")
            for u in range(PACK):
                nc.tensor.transpose(bank[:, u * P : (u + 1) * P], words[:, u, :, chunk], order[:])
            turned[n] = bank

        def empty(n):
            copy = nc.vector.tensor_copy if n == 1 else nc.scalar.copy
            if n < SIDE_UNITS:
                t, r = side_unit(n)
                if r == 0:
                    w_grouped[t] = stage.tile([P, 2, ROWS, PACK], BF16, name="w_grouped", align_bytes=64)
                target = w_grouped[t][:, :, r * P : (r + 1) * P, :]
            else:
                x_grouped[n] = stage.tile([P, 2, P, PACK], BF16, name="x_grouped", align_bytes=64, bufs=3)
                target = x_grouped[n][:]
            copy(out=target, in_=turned[n][:].bitcast(BF16).rearrange("p (u b e) -> p e b u", u=PACK, b=P, e=2))

        def quantise(n):
            if n < SIDE_UNITS:
                t, r = side_unit(n)
                if r == ROW_TILES - 1:
                    nc.vector.quantize_mx(
                        out=w_codes[:, t, :].bitcast(FP8X4),
                        scales=w_scales[:, t, :],
                        in_=w_grouped[t][:].rearrange("p e o u -> p (e o u)"),
                    )
            else:
                r, t = divmod(n - SIDE_UNITS, CHUNKS)
                nc.vector.quantize_mx(
                    out=x_codes[:, r, t, :].bitcast(FP8X4),
                    scales=x_scales[:, r, t, :],
                    in_=x_grouped[n][:].rearrange("p e b u -> p (e b u)"),
                )

        even, odd = slice(0, P), slice(P, 2 * P)
        w_even, w_odd = slice(0, ROWS), slice(ROWS, 2 * ROWS)

        def product(out, r, t, x_cols, w_cols, start, stop):
            nc.tensor.matmul_mx(
                out=out,
                lhsT=x_codes[:, r, t, x_cols].bitcast(FP8X4),
                lhsT_scale=x_scales[:, r, t, x_cols],
                rhs=w_codes[:, t, w_cols].bitcast(FP8X4),
                rhs_scale=w_scales[:, t, w_cols],
                start=start,
                stop=stop,
            )

        def products(n):
            r, t = divmod(n - SIDE_UNITS, CHUNKS)
            a = logit_pool.tile([P, 2, ROWS], F32, name="a")
            product(a[:, 0, :], r, t, even, w_odd, True, True)
            product(a[:, 1, :], r, t, even, w_even, True, False)
            product(a[:, 1, :], r, t, odd, w_odd, False, True)
            logits[n] = a

        def exponentials(n):
            r, t = divmod(n - SIDE_UNITS, CHUNKS)
            sums[n] = small.tile([P, 2], F32, name="total")
            for j in range(2):
                nc.scalar.activation(
                    out=planes[r][:, SLOTS * t + j, :],
                    in_=logits[n][:, j, :],
                    func=ACT.Exp,
                    bias=shifts[n][:, j : j + 1],
                    scale=SOFTMAX_SCALE,
                    accum_out=sums[n][:, j : j + 1],
                )

        def maxima(n):
            tops[n] = small.tile([P, 2], F32, name="top")
            nc.vector.tensor_reduce(out=tops[n][:], in_=logits[n][:], axis=AXIS.X, op=ALU.max)

        def shift(n):
            shifts[n] = small.tile([P, 2], F32, name="shift")
            nc.vector.tensor_scalar(out=shifts[n][:], in0=tops[n][:], scalar1=-SOFTMAX_SCALE, scalar2=None, op0=ALU.mult)

        def gain(n):
            gains[n] = small.tile([P, 2], F32, name="gain")
            nc.vector.reciprocal(out=gains[n][:], in_=sums[n][:])

        def divide(n):
            r, t = divmod(n - SIDE_UNITS, CHUNKS)
            for j in range(2):
                nc.vector.tensor_scalar(
                    out=planes[r][:, SLOTS * t + j, :],
                    in0=planes[r][:, SLOTS * t + j, :],
                    scalar1=gains[n][:, j : j + 1],
                    scalar2=None,
                    op0=ALU.mult,
                )

        def cast_centres(copy, r, k, h):
            o0 = h * STEP
            copy(
                out=planes[r][:].rearrange("p (t j) o -> p t j o", j=SLOTS)[:, :, SLOTS - 1, o0 : o0 + STEP].rearrange(
                    "p t (g e i) -> p t g e i", e=PAIR, i=RUN
                ),
                in_=lower_src[k][r][:, o0 * CHUNKS : (o0 + STEP) * CHUNKS].rearrange(
                    "p (g i e t) -> p t g e i", i=RUN, e=PAIR, t=CHUNKS
                ),
            )

        def lower_piece(copy, r, k, h):
            o0 = h * STEP
            filled = pieces.tile([P, STEP * WIDTH], F32, name="filled", align_bytes=DMA_ALIGN)
            copy(
                out=filled[:].rearrange("p (g i e s) -> p g e s i", i=RUN, e=PAIR, s=WIDTH),
                in_=planes[r][:, :, o0 : o0 + STEP].rearrange("p s (g e i) -> p g e s i", e=PAIR, i=RUN),
            )
            store(k, r, o0, filled)

        def step(n):
            if n < UNITS:
                empty(n)
            if 0 <= n - 1 < UNITS:
                quantise(n - 1)
                if n - 1 >= SIDE_UNITS:
                    products(n - 1)
            if n + AHEAD < UNITS:
                turn(n + AHEAD)
            if SIDE_UNITS <= n - 4 < UNITS:
                gain(n - 4)
            if SIDE_UNITS <= n - 2 < UNITS:
                maxima(n - 2)
            if SIDE_UNITS <= n - 4 < UNITS:
                divide(n - 4)
            if SIDE_UNITS <= n - 2 < UNITS:
                shift(n - 2)
            if SIDE_UNITS <= n - 3 < UNITS:
                exponentials(n - 3)
            if n in UPPER_STEPS:
                upper_piece(nc.vector.tensor_copy, 2 + UPPER_STEPS.index(n))
            for r in range(ROW_TILES):
                if 0 <= n - CENTRE_STEPS[r] < HALVES:
                    cast_centres(nc.vector.tensor_copy, r, 0, n - CENTRE_STEPS[r])
            i = n - (SIDE_UNITS + CHUNKS + 3)
            if 1 <= i < 1 + HALVES:
                cast_centres(nc.scalar.copy, 0, 1, i - 1)
            if 0 <= i < 2 * HALVES:
                lower_piece(nc.scalar.copy if i == 2 * HALVES - 1 else nc.vector.tensor_copy, 0, i // HALVES, i % HALVES)
            if n == UNITS + 3:
                lower_piece(nc.vector.tensor_copy, 1, 0, 0)
                lower_piece(nc.scalar.copy, 1, 0, 1)
                for h in range(HALVES):
                    cast_centres(nc.vector.tensor_copy, 1, 1, h)
                    lower_piece(nc.vector.tensor_copy, 1, 1, h)

        with tc.tile_pool(name="sides", bufs=1) as sides:
            for h in range(2):
                side_sb.append([sides.tile([P, C * 2 * SIDE_CHUNKS], BF16, name="side%d%d" % (h, r), align_bytes=DMA_ALIGN) for r in range(ROW_TILES)])
            load_upper(0, 0)
            for r in range(ROW_TILES):
                nc.sync.dma_start(out=side_sb[0][r][:], in_=by_row_tile(left)[r])
            load_upper(1, 0)
            for r in range(ROW_TILES):
                nc.sync.dma_start(out=side_sb[1][r][:], in_=by_row_tile(right)[r])
            load_upper(0, 1)
            load_upper(1, 1)
            nc.sync.dma_start(out=mid_sb[0][:], in_=by_row_tile(mid)[0])
            load_lower(0, 0)
            load_lower(0, 1)
            nc.sync.dma_start(out=mid_sb[1][:], in_=by_row_tile(mid)[1])
            upper_piece(nc.vector.tensor_copy, 0)
            upper_piece(nc.scalar.copy, 1)
            load_lower(1, 0)
            load_lower(1, 1)
            for n in range(AHEAD):
                turn(n)
            for n in range(SIDE_UNITS - AHEAD):
                step(n)
        planes_pool = ctx.enter_context(tc.tile_pool(name="planes_pool", bufs=1))
        for r in range(ROW_TILES):
            planes.append(planes_pool.tile([P, WIDTH, ROWS], F32, name="planes%d" % r))
        for n in range(SIDE_UNITS - AHEAD, UNITS + 4):
            step(n)
